import numpy as np
import ml_dtypes


def mxq(x, axis, fmt="e4m3"):
    dtype, down = {"e4m3": (ml_dtypes.float8_e4m3fn, 7), "e5m2": (ml_dtypes.float8_e5m2, 14)}[fmt]
    v = np.moveaxis(np.asarray(x, np.float32).astype(ml_dtypes.bfloat16).astype(np.float64), axis, -1)
    blocks = v.reshape(v.shape[:-1] + (-1, 32))
    amax = np.abs(blocks).max(-1, keepdims=True)
    byte = np.maximum(np.where(amax > 0, np.frexp(amax)[1] - 1 + 127, 0) - down, 1)
    scale = np.exp2(byte - 127.0)
    codes = (blocks / scale).astype(np.float32).astype(dtype).astype(np.float64)
    return np.moveaxis((codes * scale).reshape(v.shape), -1, axis)


WIDE = False


def mx_kscale(k):
    if not WIDE:
        return np.ones(k)
    levels = np.array([10, -10, 5, -5, 0])
    if k % 512:
        return np.exp2(np.random.permutation(np.resize(levels, k // 32))).repeat(32)
    a = np.empty((k // 512, 16))
    for p in range(k // 512):
        a[p, :8] = np.random.permutation(np.resize(levels, 8))
        for g in range(8):
            far = levels[np.abs(levels - a[p, g]) >= 10]
            a[p, g + 8] = far[np.random.randint(len(far))]
    return np.exp2(a.ravel()).repeat(32)


BF16 = ml_dtypes.bfloat16


def bf(x):
    return np.asarray(x, np.float32).astype(BF16)


def f64(x):
    return np.asarray(x).astype(np.float64)


B, S, D, E, HD = 2, 512, 512, 512, 64
ROPE_BASE = 10000.0


def rope_tables():
    inv_freq = 1.0 / ROPE_BASE ** (np.arange(0, E, 2) / E)
    ang = np.repeat(np.arange(S)[:, None] * inv_freq[None, :], 2, axis=-1)
    return np.cos(ang), np.sin(ang)


def rotate_half(v):
    h = v.shape[-1] // 2
    return np.concatenate([-v[..., h:], v[..., :h]], axis=-1)


def draw0():
    s = mx_kscale(D)
    return {"x": bf(np.random.standard_normal((B, S, D)) * s),
            "Wq": bf(np.random.standard_normal((D, E)) * 0.5 / np.sqrt(D) / s[:, None]),
            "bq": bf(np.random.standard_normal(E) * 0.1),
            "Wk": bf(np.random.standard_normal((D, E)) * 0.5 / np.sqrt(D) / s[:, None]),
            "bk": bf(np.random.standard_normal(E) * 0.1)}


def core(x, Wq, bq, Wk, bk):
    xq = mxq(f64(x), 2, "e4m3")
    q = (xq @ mxq(f64(Wq), 0, "e4m3")) + f64(bq)
    k = (xq @ mxq(f64(Wk), 0, "e4m3")) + f64(bk)
    cos, sin = rope_tables()
    qr = q * cos + rotate_half(q) * sin
    kr = k * cos + rotate_half(k) * sin
    return qr, kr


def e4m3fn_bytes(y):
    return np.clip(np.asarray(y, np.float64), -448.0, 448.0).astype(np.float32).astype(ml_dtypes.float8_e4m3fn).view(np.uint8)


def e4m3fn_values(b):
    return np.asarray(b, np.uint8).view(ml_dtypes.float8_e4m3fn).astype(np.float64)


def setup_inputs():
    d = draw0()
    x0 = np.asarray(d['x']).astype(np.float64)
    s = (np.max(np.abs(x0), axis=(0, 1), keepdims=True) / 448.0).astype(np.float32)
    out = {}
    for k, v in d.items():
        if k == 'x':
            out['x_bytes'] = e4m3fn_bytes(x0 / s.astype(np.float64))
            out['x_scale'] = s
        else:
            out[k] = v
    return out


def reference(x_bytes, x_scale, Wq, bq, Wk, bk):
    return core(e4m3fn_values(x_bytes) * x_scale.astype(np.float64), Wq, bq, Wk, bk)

@@ -1,0 +1,300 @@
+import math
+from contextlib import ExitStack
+
+import concourse.mybir as mybir
+from concourse.masks import make_identity
+
+F32 = mybir.dt.float32
+BF16 = mybir.dt.bfloat16
+U8 = mybir.dt.uint8
+U32 = mybir.dt.uint32
+I32 = mybir.dt.int32
+FP8 = mybir.dt.float8_e4m3fn
+FP8X4 = mybir.dt.float8_e4m3fn_x4
+ALU = mybir.AluOpType
+ACT = mybir.ActivationFunctionType
+
+P = 128
+S = 512
+FLOPS = 2 * 1024 * 512 * 1024
+
+TWO_PI = 2.0 * math.pi
+RATIO = 10000.0 ** (-1.0 / 256.0)
+
+STEEP = 3
+LATE = 448
+GROUPS = ((0, 0), (0, 1), (1, 0), (1, 1))
+TILES = ((0, 0), (1, 0), (0, 1), (1, 1))
+ON_POOL = ((0, 1), (0, 1), (0, 1), (0, 1))
+
+
+def tile_ropemultiheadattention_pa_kernel(tc, x_bytes, x_scale, Wq, bq, Wk, bk, out_0, out_1):
+    nc = tc.nc
+    weights = (Wq, Wk)
+    biases = (bq, bk)
+    outs = (out_0, out_1)
+
+    with ExitStack() as ctx:
+        keep = ctx.enter_context(tc.tile_pool(name="keep", bufs=1))
+        work = ctx.enter_context(tc.tile_pool(name="work", bufs=3))
+        prod = ctx.enter_context(tc.tile_pool(name="prod", bufs=8))
+        resp = ctx.enter_context(tc.tile_pool(name="resp", bufs=8))
+        psP = ctx.enter_context(tc.psum_pool(name="psP", bufs=5))
+        psO = ctx.enter_context(tc.psum_pool(name="psO", bufs=3))
+        ctx.enter_context(tc.manual_schedule())
+
+        xs4 = keep.tile([P, 4], F32, name="xs4")
+        nc.scalar.dma_start(out=xs4[:], in_=x_scale.rearrange("a b (p t) -> (a b p) t", t=4))
+        xv = x_bytes.rearrange("b (a p) k -> b p a k", p=P)
+        xbytes = [keep.tile([P, 4, 512], U8, name="xbytes%d" % b) for b in range(2)]
+        wraw = [keep.tile([P, 4, 512], BF16, name="wraw%d" % x) for x in range(2)]
+        nc.sync.dma_start(out=xbytes[0][:], in_=xv[0])
+        nc.sync.dma_start(out=wraw[0][:], in_=weights[0].rearrange("(p j) w -> p j w", j=4))
+        nc.sync.dma_start(out=xbytes[1][:], in_=xv[1])
+        nc.sync.dma_start(out=wraw[1][:], in_=weights[1].rearrange("(p j) w -> p j w", j=4))
+        bias = [keep.tile([P, 2, 2], BF16, name="bias%d" % x) for x in range(2)]
+        for x in range(2):
+            nc.scalar.dma_start(out=bias[x][:], in_=biases[x].rearrange("(h p r) -> p h r", h=2, r=2))
+
+        tabs = [keep.tile([P, 2, S], F32, name="tabs%d" % hf) for hf in range(2)]
+        warm = keep.tile([P, 1], F32, name="warm")
+        nc.gpsimd.memset(warm[:], 0.0)
+        warm2 = keep.tile([P, 1], F32, name="warm2")
+        nc.scalar.activation(out=warm2[:], in_=warm[:], func=ACT.Sin)
+        ident = keep.tile([P, P], F32, name="ident")
+        make_identity(nc, ident[:])
+        pos = keep.tile([P, S], F32, name="pos")
+        nc.gpsimd.iota(pos[:], pattern=[[1, S]], base=0, channel_multiplier=0, allow_small_or_imprecise_dtypes=True)
+        nc.gpsimd.memset(tabs[0][:, 1, 0:1], 0.0)
+        row = keep.tile([P, 1], F32, name="row")
+        nc.gpsimd.iota(row[:], pattern=[[0, 1]], base=0, channel_multiplier=1, allow_small_or_imprecise_dtypes=True)
+
+        xs = keep.tile([P, 512], F32, name="xs")
+        spread = psO.tile([P, 4, P], F32, name="spread", tag="O")
+        for t in range(4):
+            nc.tensor.transpose(spread[:, t, :], xs4[:, t:t + 1].to_broadcast([P, P]), ident[:])
+
+        powers = keep.tile([P, P], F32, name="powers")
+        probe = keep.tile([P, 1], F32, name="probe")
+        probe_i = keep.tile([P, 1], I32, name="probe_i")
+        shift = keep.tile([P, 2], F32, name="shift")
+        nc.vector.memset(powers[:, 0:1], 1.0)
+        nc.vector.memset(probe[:], 0.75)
+
+        def level(n, count):
+            for m in range(1, count + 1):
+                nc.vector.tensor_scalar(out=powers[:, m * n:(m + 1) * n], in0=powers[:, 0:n], scalar1=RATIO ** (m * n), scalar2=None, op0=ALU.mult)
+
+        level(1, 3)
+        nc.vector.tensor_scalar(out=probe_i[:], in0=probe[:], scalar1=1.0, scalar2=0.0, op0=ALU.mult, op1=ALU.add)
+        level(4, 3)
+        nc.vector.tensor_scalar(out=shift[:, 0:1], in0=probe_i[:], scalar1=-0.5, scalar2=0.5, op0=ALU.mult, op1=ALU.add)
+        nc.vector.tensor_scalar(out=shift[:, 1:2], in0=probe_i[:], scalar1=-0.5, scalar2=0.75, op0=ALU.mult, op1=ALU.add)
+        level(16, 3)
+        level(64, 1)
+        diag = keep.tile([P, P], F32, name="diag")
+        turns = keep.tile([P, 3], F32, name="turns")
+        nc.vector.scalar_tensor_tensor(out=diag[:], in0=powers[:], scalar=1.0 / TWO_PI, in1=ident[:], op0=ALU.mult, op1=ALU.mult, accum_out=turns[:, 0:1])
+        nc.vector.tensor_scalar(out=turns[:, 2:3], in0=turns[:, 0:1], scalar1=-TWO_PI * RATIO ** 128, scalar2=None, op0=ALU.mult)
+        nc.vector.tensor_scalar(out=turns[:, 1:2], in0=turns[:, 0:1], scalar1=RATIO ** 128, scalar2=None, op0=ALU.mult)
+        late = keep.tile([P, 3], F32, name="late")
+        nc.vector.tensor_scalar(out=late[:, 0:1], in0=row[:], scalar1=float(STEEP), scalar2=2.0, op0=ALU.is_ge, op1=ALU.mult)
+        nc.vector.tensor_scalar(out=late[:, 1:2], in0=late[:, 0:1], scalar1=1.0, scalar2=turns[:, 2:3], op0=ALU.subtract, op1=ALU.mult)
+        nc.vector.tensor_scalar(out=late[:, 2:3], in0=late[:, 0:1], scalar1=math.pi, scalar2=-1.5 * math.pi, op0=ALU.mult, op1=ALU.add)
+
+        nc.scalar.activation(out=tabs[0][:, 1, 1:S], in_=pos[:, 1:S], func=ACT.Sin, scale=turns[:, 2:3], bias=math.pi)
+        nc.scalar.copy(out=xs[:].rearrange("p (n t) -> p n t", t=4), in_=spread[:].rearrange("p t n -> p n t"))
+
+        def cosine_upper():
+            nc.scalar.activation(out=tabs[1][:, 0, 0:LATE], in_=pos[:, 0:LATE], func=ACT.Sin, scale=turns[:, 2:3], bias=0.5 * math.pi)
+            nc.scalar.activation(out=tabs[1][:, 0, LATE:S], in_=pos[:, LATE:S], func=ACT.Sin, scale=late[:, 1:2], bias=late[:, 2:3])
+
+        wholes = {}
+        fracs = {}
+
+        def whole_turns(kind, hf):
+            whole = work.tile([P, S], I32, name="whole", tag="whole")
+            nc.vector.tensor_scalar(out=whole[:], in0=pos[:], scalar1=turns[:, hf:hf + 1], scalar2=shift[:, kind:kind + 1], op0=ALU.mult, op1=ALU.add)
+            wholes[(kind, hf)] = whole
+
+        def fraction(kind, hf):
+            frac = work.tile([P, S], F32, name="frac", tag="frac")
+            nc.vector.scalar_tensor_tensor(out=frac[:], in0=pos[:], scalar=turns[:, hf:hf + 1], in1=wholes[(kind, hf)][:], op0=ALU.mult, op1=ALU.subtract)
+            fracs[(kind, hf)] = frac
+
+        def sine(kind, hf):
+            if kind == 1:
+                nc.scalar.activation(out=tabs[hf][:, 0, :], in_=fracs[(kind, hf)][:], func=ACT.Sin, scale=TWO_PI, bias=0.5 * math.pi)
+            else:
+                nc.scalar.activation(out=tabs[1 - hf][:, 1, :], in_=fracs[(kind, hf)][:], func=ACT.Sin, scale=-TWO_PI)
+
+        xw = [keep.tile([P, 4, 512], BF16, name="xw%d" % b) for b in range(2)]
+        xg = [keep.tile([P, 2048], BF16, name="xg%d" % b, align_bytes=64) for b in range(2)]
+        xc = [keep.tile([P, 512], U32, name="xc%d" % b, align_bytes=64) for b in range(2)]
+        xsc = [keep.tile([P, 512], U8, name="xsc%d" % b, align_bytes=64) for b in range(2)]
+        turned = {}
+
+        def widen(b, a):
+            nc.vector.tensor_tensor(out=xw[b][:, a, :], in0=xbytes[b][:, a, :].bitcast(FP8), in1=xs[:], op=ALU.mult)
+
+        def turn_x(b, h):
+            if b == 0:
+                xt = psO.tile([P, 2, 2, P], F32, name="xt", tag="O")
+            else:
+                xt = psP.tile([P, 2, 2, P], F32, name="xt1", tag="P")
+            for a in range(2):
+                words = xw[b][:, 2 * h + a, :].bitcast(F32)
+                for u in range(2):
+                    nc.tensor.transpose(xt[:, a, u, :], words[:, u:256:2], ident[:])
+            turned[(b, h)] = xt
+
+        def take_x(b, h):
+            nc.scalar.copy(
+                out=xg[b][:].bitcast(F32)[:, h * 512:(h + 1) * 512].rearrange("p (a r u) -> p a r u", a=2, u=2),
+                in_=turned[(b, h)][:].rearrange("p a u r -> p a r u"),
+            )
+
+        def quant_x(b):
+            nc.vector.quantize_mx(out=xc[b][:].bitcast(FP8X4), scales=xsc[b][:], in_=xg[b][:])
+
+        wg = [keep.tile([P, 2048], BF16, name="wg%d" % x, align_bytes=64) for x in range(2)]
+        wc = [keep.tile([P, 512], U32, name="wc%d" % x, align_bytes=64) for x in range(2)]
+        wsc = [keep.tile([P, 512], U8, name="wsc%d" % x, align_bytes=64) for x in range(2)]
+
+        def prep_w(x, pars=(0, 1)):
+            for par in pars:
+                for hf in range(2):
+                    cb = 2 * par + hf
+                    nc.scalar.copy(
+                        out=wg[x][:, cb * 512:(cb + 1) * 512].rearrange("p (q j) -> p q j", j=4),
+                        in_=wraw[x][:, :, 256 * hf + par:256 * hf + 256:2].rearrange("p j q -> p q j"),
+                    )
+
+        def quant_w(x):
+            nc.vector.quantize_mx(out=wc[x][:].bitcast(FP8X4), scales=wsc[x][:], in_=wg[x][:])
+
+        acc = {}
+        terms = {}
+        banks = {}
+        moveds = {}
+
+        def project(g, which):
+            x, b = GROUPS[g]
+            for par, hf in which:
+                cb = 2 * par + hf
+                pt = psP.tile([P, S], F32, name="pt", tag="P")
+                nc.tensor.matmul_mx(
+                    out=pt[:],
+                    lhsT=wc[x][:, cb * P:(cb + 1) * P].bitcast(FP8X4),
+                    lhsT_scale=wsc[x][:, cb * P:(cb + 1) * P],
+                    rhs=xc[b][:].bitcast(FP8X4),
+                    rhs_scale=xsc[b][:],
+                    start=True,
+                    stop=True,
+                )
+                acc[(g, par, hf)] = pt
+
+        def new_terms(g, par, hf):
+            mf = prod.tile([P, 2, S], F32, name="mf", tag="m")
+            terms[(g, par, hf)] = mf
+            return mf
+
+        def rotate(g, par, hf, lo=0, hi=S):
+            x, b = GROUPS[g]
+            if lo == 0:
+                new_terms(g, par, hf)
+            mf = terms[(g, par, hf)]
+            nc.vector.scalar_tensor_tensor(
+                out=mf[:, :, lo:hi],
+                in0=acc[(g, par, hf)][:, lo:hi].unsqueeze(1).to_broadcast([P, 2, hi - lo]),
+                scalar=bias[x][:, hf, par:par + 1],
+                in1=tabs[hf][:, :, lo:hi],
+                op0=ALU.add,
+                op1=ALU.mult,
+            )
+
+        def move(g, par, hf):
+            x, b = GROUPS[g]
+            moved = work.tile([P, S], F32, name="moved", tag="moved")
+            nc.scalar.activation(out=moved[:], in_=acc[(g, par, hf)][:], func=ACT.Identity, bias=bias[x][:, hf, par:par + 1], scale=1.0)
+            moveds[g] = moved
+
+        def rotate_pool(g, par, hf):
+            mf = new_terms(g, par, hf)
+            for w in ON_POOL[g]:
+                nc.gpsimd.tensor_tensor(out=mf[:, w, :], in0=moveds[g][:], in1=tabs[hf][:, w, :], op=ALU.mult)
+
+        def rotate_one(g, par, hf, w):
+            x, b = GROUPS[g]
+            nc.vector.scalar_tensor_tensor(
+                out=terms[(g, par, hf)][:, w, :],
+                in0=acc[(g, par, hf)][:],
+                scalar=bias[x][:, hf, par:par + 1],
+                in1=tabs[hf][:, w, :],
+                op0=ALU.add,
+                op1=ALU.mult,
+            )
+
+        def back(g, par, tt):
+            if par == 0:
+                banks[(g, tt)] = psO.tile([P, S], F32, name="ot", tag="O")
+            ot = banks[(g, tt)]
+            for hf in range(2):
+                c0 = (2 * hf + par) * P
+                nc.tensor.matmul(out=ot[:, c0:c0 + P], lhsT=terms[(g, par, hf)][:, 0, tt * P:(tt + 1) * P], rhs=ident[:], is_transpose=True, start=True, stop=False)
+                nc.tensor.matmul(out=ot[:, c0:c0 + P], lhsT=terms[(g, par, 1 - hf)][:, 1, tt * P:(tt + 1) * P], rhs=ident[:], is_transpose=True, start=False, stop=True)
+
+        def store(g, tt, on_vector=False):
+            x, b = GROUPS[g]
+            res = resp.tile([P, S], F32, name="res", tag="res")
+            copy = nc.vector.tensor_copy if on_vector else nc.scalar.copy
+            copy(
+                out=res[:].rearrange("p (h q r) -> p h q r", h=2, r=2),
+                in_=banks[(g, tt)][:].rearrange("p (h r q) -> p h q r", h=2, r=2),
+            )
+            nc.sync.dma_start(out=outs[x][b, tt * P:(tt + 1) * P, :], in_=res[:])
+
+        whole_turns(1, 0)
+        whole_turns(0, 0)
+        fraction(1, 0)
+        fraction(0, 0)
+        cosine_upper()
+        sine(1, 0)
+        sine(0, 0)
+        for b in range(2):
+            for a in range(4):
+                widen(b, a)
+                if a % 2 == 1:
+                    turn_x(b, a // 2)
+        prep_w(0)
+        take_x(0, 0)
+        take_x(0, 1)
+        take_x(1, 0)
+        take_x(1, 1)
+        quant_w(0)
+        quant_x(0)
+        project(0, TILES)
+        quant_x(1)
+
+        move(0, 1, 0)
+        for g in range(4):
+            rotate_pool(g, 1, 0)
+            rotate(g, 0, 0)
+            if g == 0:
+                prep_w(1, (0,))
+                project(1, TILES[0:3])
+                move(1, 1, 0)
+                prep_w(1, (1,))
+            if g == 1:
+                quant_w(1)
+            rotate(g, 0, 1)
+            if g == 0:
+                project(1, TILES[3:4])
+            elif g < 3:
+                project(g + 1, TILES)
+                move(g + 1, 1, 0)
+            rotate(g, 1, 1)
+            for tt in range(4):
+                back(g, 0, tt)
+                back(g, 1, tt)
+                store(g, tt)

@@ -58,16 +58,14 @@ def tile_ropemultiheadattention_pa_kernel(tc, x_bytes, x_scale, Wq, bq, Wk, bk, 
 
         tabs = [keep.tile([P, 2, S], F32, name="tabs%d" % hf) for hf in range(2)]
         warm = keep.tile([P, 1], F32, name="warm")
-        nc.gpsimd.memset(warm[:], 0.0)
+        nc.vector.memset(warm[:], 0.0)
         warm2 = keep.tile([P, 1], F32, name="warm2")
         nc.scalar.activation(out=warm2[:], in_=warm[:], func=ACT.Sin)
         ident = keep.tile([P, P], F32, name="ident")
         make_identity(nc, ident[:])
         pos = keep.tile([P, S], F32, name="pos")
         nc.gpsimd.iota(pos[:], pattern=[[1, S]], base=0, channel_multiplier=0, allow_small_or_imprecise_dtypes=True)
-        nc.gpsimd.memset(tabs[0][:, 1, 0:1], 0.0)
-        row = keep.tile([P, 1], F32, name="row")
-        nc.gpsimd.iota(row[:], pattern=[[0, 1]], base=0, channel_multiplier=1, allow_small_or_imprecise_dtypes=True)
+        nc.vector.memset(tabs[0][:, 1, 0:1], 0.0)
 
         xs = keep.tile([P, 512], F32, name="xs")
         spread = psO.tile([P, 4, P], F32, name="spread", tag="O")
@@ -98,7 +96,7 @@ def tile_ropemultiheadattention_pa_kernel(tc, x_bytes, x_scale, Wq, bq, Wk, bk, 
         nc.vector.tensor_scalar(out=turns[:, 2:3], in0=turns[:, 0:1], scalar1=-TWO_PI * RATIO ** 128, scalar2=None, op0=ALU.mult)
         nc.vector.tensor_scalar(out=turns[:, 1:2], in0=turns[:, 0:1], scalar1=RATIO ** 128, scalar2=None, op0=ALU.mult)
         late = keep.tile([P, 3], F32, name="late")
-        nc.vector.tensor_scalar(out=late[:, 0:1], in0=row[:], scalar1=float(STEEP), scalar2=2.0, op0=ALU.is_ge, op1=ALU.mult)
+        nc.vector.tensor_scalar(out=late[:, 0:1], in0=turns[:, 0:1], scalar1=RATIO ** (STEEP - 0.5) / TWO_PI, scalar2=2.0, op0=ALU.is_le, op1=ALU.mult)
         nc.vector.tensor_scalar(out=late[:, 1:2], in0=late[:, 0:1], scalar1=1.0, scalar2=turns[:, 2:3], op0=ALU.subtract, op1=ALU.mult)
         nc.vector.tensor_scalar(out=late[:, 2:3], in0=late[:, 0:1], scalar1=math.pi, scalar2=-1.5 * math.pi, op0=ALU.mult, op1=ALU.add)
 

@@ -252,6 +252,19 @@ def tile_ropemultiheadattention_pa_kernel(tc, x_bytes, x_scale, Wq, bq, Wk, bk, 
             )
             nc.sync.dma_start(out=outs[x][b, tt * P:(tt + 1) * P, :], in_=res[:])
 
+        def last_tile(g, tt):
+            x, b = GROUPS[g]
+            for hf in range(2):
+                oh = psO.tile([P, 2 * P], F32, name="oh", tag="O")
+                for par in range(2):
+                    c0 = par * P
+                    nc.tensor.matmul(out=oh[:, c0:c0 + P], lhsT=terms[(g, par, hf)][:, 0, tt * P:(tt + 1) * P], rhs=ident[:], is_transpose=True, start=True, stop=False)
+                    nc.tensor.matmul(out=oh[:, c0:c0 + P], lhsT=terms[(g, par, 1 - hf)][:, 1, tt * P:(tt + 1) * P], rhs=ident[:], is_transpose=True, start=False, stop=True)
+                resh = resp.tile([P, 2 * P], F32, name="resh", tag="res")
+                copy = nc.vector.tensor_copy if hf == 1 else nc.scalar.copy
+                copy(out=resh[:].rearrange("p (q r) -> p q r", r=2), in_=oh[:].rearrange("p (r q) -> p q r", r=2))
+                nc.sync.dma_start(out=outs[x][b, tt * P:(tt + 1) * P, 2 * P * hf:2 * P * (hf + 1)], in_=resh[:])
+
         whole_turns(1, 0)
         whole_turns(0, 0)
         fraction(1, 0)
@@ -293,6 +306,9 @@ def tile_ropemultiheadattention_pa_kernel(tc, x_bytes, x_scale, Wq, bq, Wk, bk, 
                 move(g + 1, 1, 0)
             rotate(g, 1, 1)
             for tt in range(4):
-                back(g, 0, tt)
-                back(g, 1, tt)
-                store(g, tt)
+                if g == 3 and tt == 3:
+                    last_tile(g, tt)
+                else:
+                    back(g, 0, tt)
+                    back(g, 1, tt)
+                    store(g, tt)

@@ -164,8 +164,8 @@ def tile_ropemultiheadattention_pa_kernel(tc, x_bytes, x_scale, Wq, bq, Wk, bk, 
                 for hf in range(2):
                     cb = 2 * par + hf
                     nc.scalar.copy(
-                        out=wg[x][:, cb * 512:(cb + 1) * 512].rearrange("p (q j) -> p q j", j=4),
-                        in_=wraw[x][:, :, 256 * hf + par:256 * hf + 256:2].rearrange("p j q -> p q j"),
+                        out=wg[x][:, cb * 512:(cb + 1) * 512].rearrange("p (c i j) -> p c j i", i=4, j=4),
+                        in_=wraw[x][:, :, 256 * hf + par:256 * hf + 256:2].rearrange("p j (c i) -> p c j i", i=4),
                     )
 
         def quant_w(x):

@@ -101,7 +101,6 @@ def tile_ropemultiheadattention_pa_kernel(tc, x_bytes, x_scale, Wq, bq, Wk, bk, 
         nc.vector.tensor_scalar(out=late[:, 2:3], in0=late[:, 0:1], scalar1=math.pi, scalar2=-1.5 * math.pi, op0=ALU.mult, op1=ALU.add)
 
         nc.scalar.activation(out=tabs[0][:, 1, 1:S], in_=pos[:, 1:S], func=ACT.Sin, scale=turns[:, 2:3], bias=math.pi)
-        nc.scalar.copy(out=xs[:].rearrange("p (n t) -> p n t", t=4), in_=spread[:].rearrange("p t n -> p n t"))
 
         def cosine_upper():
             nc.scalar.activation(out=tabs[1][:, 0, 0:LATE], in_=pos[:, 0:LATE], func=ACT.Sin, scale=turns[:, 2:3], bias=0.5 * math.pi)
@@ -269,6 +268,7 @@ def tile_ropemultiheadattention_pa_kernel(tc, x_bytes, x_scale, Wq, bq, Wk, bk, 
         whole_turns(0, 0)
         fraction(1, 0)
         fraction(0, 0)
+        nc.vector.tensor_copy(out=xs[:].rearrange("p (n t) -> p n t", t=4), in_=spread[:].rearrange("p t n -> p n t"))
         cosine_upper()
         sine(1, 0)
         sine(0, 0)

@@ -21,7 +21,6 @@ FLOPS = 2 * 1024 * 512 * 1024
 TWO_PI = 2.0 * math.pi
 RATIO = 10000.0 ** (-1.0 / 256.0)
 
-STEEP = 3
 LATE = 448
 GROUPS = ((0, 0), (0, 1), (1, 0), (1, 1))
 TILES = ((0, 0), (1, 0), (0, 1), (1, 1))
@@ -44,7 +43,7 @@ def tile_ropemultiheadattention_pa_kernel(tc, x_bytes, x_scale, Wq, bq, Wk, bk, 
         ctx.enter_context(tc.manual_schedule())
 
         xs4 = keep.tile([P, 4], F32, name="xs4")
-        nc.scalar.dma_start(out=xs4[:], in_=x_scale.rearrange("a b (p t) -> (a b p) t", t=4))
+        nc.sync.dma_start(out=xs4[:], in_=x_scale.rearrange("a b (p t) -> (a b p) t", t=4))
         xv = x_bytes.rearrange("b (a p) k -> b p a k", p=P)
         xbytes = [keep.tile([P, 4, 512], U8, name="xbytes%d" % b) for b in range(2)]
         wraw = [keep.tile([P, 4, 512], BF16, name="wraw%d" % x) for x in range(2)]
@@ -75,7 +74,7 @@ def tile_ropemultiheadattention_pa_kernel(tc, x_bytes, x_scale, Wq, bq, Wk, bk, 
         powers = keep.tile([P, P], F32, name="powers")
         probe = keep.tile([P, 1], F32, name="probe")
         probe_i = keep.tile([P, 1], I32, name="probe_i")
-        shift = keep.tile([P, 2], F32, name="shift")
+        shift = keep.tile([P, 1], F32, name="shift")
         nc.vector.memset(powers[:, 0:1], 1.0)
         nc.vector.memset(probe[:], 0.75)
 
@@ -87,43 +86,38 @@ def tile_ropemultiheadattention_pa_kernel(tc, x_bytes, x_scale, Wq, bq, Wk, bk, 
         nc.vector.tensor_scalar(out=probe_i[:], in0=probe[:], scalar1=1.0, scalar2=0.0, op0=ALU.mult, op1=ALU.add)
         level(4, 3)
         nc.vector.tensor_scalar(out=shift[:, 0:1], in0=probe_i[:], scalar1=-0.5, scalar2=0.5, op0=ALU.mult, op1=ALU.add)
-        nc.vector.tensor_scalar(out=shift[:, 1:2], in0=probe_i[:], scalar1=-0.5, scalar2=0.75, op0=ALU.mult, op1=ALU.add)
         level(16, 3)
         level(64, 1)
         diag = keep.tile([P, P], F32, name="diag")
-        turns = keep.tile([P, 3], F32, name="turns")
+        turns = keep.tile([P, 2], F32, name="turns")
         nc.vector.scalar_tensor_tensor(out=diag[:], in0=powers[:], scalar=1.0 / TWO_PI, in1=ident[:], op0=ALU.mult, op1=ALU.mult, accum_out=turns[:, 0:1])
-        nc.vector.tensor_scalar(out=turns[:, 2:3], in0=turns[:, 0:1], scalar1=-TWO_PI * RATIO ** 128, scalar2=None, op0=ALU.mult)
-        nc.vector.tensor_scalar(out=turns[:, 1:2], in0=turns[:, 0:1], scalar1=RATIO ** 128, scalar2=None, op0=ALU.mult)
-        late = keep.tile([P, 3], F32, name="late")
-        nc.vector.tensor_scalar(out=late[:, 0:1], in0=turns[:, 0:1], scalar1=RATIO ** (STEEP - 0.5) / TWO_PI, scalar2=2.0, op0=ALU.is_le, op1=ALU.mult)
-        nc.vector.tensor_scalar(out=late[:, 1:2], in0=late[:, 0:1], scalar1=1.0, scalar2=turns[:, 2:3], op0=ALU.subtract, op1=ALU.mult)
-        nc.vector.tensor_scalar(out=late[:, 2:3], in0=late[:, 0:1], scalar1=math.pi, scalar2=-1.5 * math.pi, op0=ALU.mult, op1=ALU.add)
+        nc.vector.tensor_scalar(out=turns[:, 1:2], in0=turns[:, 0:1], scalar1=-TWO_PI * RATIO ** 128, scalar2=None, op0=ALU.mult)
 
-        nc.scalar.activation(out=tabs[0][:, 1, 1:S], in_=pos[:, 1:S], func=ACT.Sin, scale=turns[:, 2:3], bias=math.pi)
+        nc.scalar.activation(out=tabs[0][:, 1, 1:S], in_=pos[:, 1:S], func=ACT.Sin, scale=turns[:, 1:2], bias=math.pi)
+
+        beyond = keep.tile([P, S - LATE], F32, name="beyond")
 
         def cosine_upper():
-            nc.scalar.activation(out=tabs[1][:, 0, 0:LATE], in_=pos[:, 0:LATE], func=ACT.Sin, scale=turns[:, 2:3], bias=0.5 * math.pi)
-            nc.scalar.activation(out=tabs[1][:, 0, LATE:S], in_=pos[:, LATE:S], func=ACT.Sin, scale=late[:, 1:2], bias=late[:, 2:3])
+            nc.scalar.activation(out=tabs[1][:, 0, 0:LATE], in_=pos[:, 0:LATE], func=ACT.Sin, scale=turns[:, 1:2], bias=0.5 * math.pi)
+            nc.scalar.activation(out=beyond[:], in_=pos[:, LATE:S], func=ACT.Abs, scale=turns[:, 1:2], bias=math.pi)
+            nc.scalar.activation(out=tabs[1][:, 0, LATE:S], in_=beyond[:], func=ACT.Sin, bias=-0.5 * math.pi)
 
-        wholes = {}
-        fracs = {}
+        whole = keep.tile([P, S], I32, name="whole")
+        frac = keep.tile([P, S], F32, name="frac")
+        folded = keep.tile([P, S], F32, name="folded")
 
-        def whole_turns(kind, hf):
-            whole = work.tile([P, S], I32, name="whole", tag="whole")
-            nc.vector.tensor_scalar(out=whole[:], in0=pos[:], scalar1=turns[:, hf:hf + 1], scalar2=shift[:, kind:kind + 1], op0=ALU.mult, op1=ALU.add)
-            wholes[(kind, hf)] = whole
+        def fractions():
+            nc.vector.tensor_scalar(out=whole[:], in0=pos[:], scalar1=turns[:, 0:1], scalar2=shift[:], op0=ALU.mult, op1=ALU.add)
+            nc.vector.scalar_tensor_tensor(out=frac[:], in0=pos[:], scalar=turns[:, 0:1], in1=whole[:], op0=ALU.mult, op1=ALU.subtract)
 
-        def fraction(kind, hf):
-            frac = work.tile([P, S], F32, name="frac", tag="frac")
-            nc.vector.scalar_tensor_tensor(out=frac[:], in0=pos[:], scalar=turns[:, hf:hf + 1], in1=wholes[(kind, hf)][:], op0=ALU.mult, op1=ALU.subtract)
-            fracs[(kind, hf)] = frac
+        def fold():
+            nc.scalar.activation(out=folded[:], in_=frac[:], func=ACT.Abs)
 
-        def sine(kind, hf):
-            if kind == 1:
-                nc.scalar.activation(out=tabs[hf][:, 0, :], in_=fracs[(kind, hf)][:], func=ACT.Sin, scale=TWO_PI, bias=0.5 * math.pi)
-            else:
-                nc.scalar.activation(out=tabs[1 - hf][:, 1, :], in_=fracs[(kind, hf)][:], func=ACT.Sin, scale=-TWO_PI)
+        def cosine_lower():
+            nc.scalar.activation(out=tabs[0][:, 0, :], in_=folded[:], func=ACT.Sin, scale=-TWO_PI, bias=0.5 * math.pi)
+
+        def sine_lower():
+            nc.scalar.activation(out=tabs[1][:, 1, :], in_=frac[:], func=ACT.Sin, scale=-TWO_PI)
 
         xw = [keep.tile([P, 4, 512], BF16, name="xw%d" % b) for b in range(2)]
         xg = [keep.tile([P, 2048], BF16, name="xg%d" % b, align_bytes=64) for b in range(2)]
@@ -264,14 +258,9 @@ def tile_ropemultiheadattention_pa_kernel(tc, x_bytes, x_scale, Wq, bq, Wk, bk, 
                 copy(out=resh[:].rearrange("p (q r) -> p q r", r=2), in_=oh[:].rearrange("p (r q) -> p q r", r=2))
                 nc.sync.dma_start(out=outs[x][b, tt * P:(tt + 1) * P, 2 * P * hf:2 * P * (hf + 1)], in_=resh[:])
 
-        whole_turns(1, 0)
-        whole_turns(0, 0)
-        fraction(1, 0)
-        fraction(0, 0)
+        fractions()
         nc.vector.tensor_copy(out=xs[:].rearrange("p (n t) -> p n t", t=4), in_=spread[:].rearrange("p t n -> p n t"))
         cosine_upper()
-        sine(1, 0)
-        sine(0, 0)
         for b in range(2):
             for a in range(4):
                 widen(b, a)
@@ -279,9 +268,12 @@ def tile_ropemultiheadattention_pa_kernel(tc, x_bytes, x_scale, Wq, bq, Wk, bk, 
                     turn_x(b, a // 2)
         prep_w(0)
         take_x(0, 0)
+        fold()
         take_x(0, 1)
+        cosine_lower()
         take_x(1, 0)
         take_x(1, 1)
+        sine_lower()
         quant_w(0)
         quant_x(0)
         project(0, TILES)

@@ -94,6 +94,7 @@ def tile_ropemultiheadattention_pa_kernel(tc, x_bytes, x_scale, Wq, bq, Wk, bk, 
         nc.vector.tensor_scalar(out=turns[:, 1:2], in0=turns[:, 0:1], scalar1=-TWO_PI * RATIO ** 128, scalar2=None, op0=ALU.mult)
 
         nc.scalar.activation(out=tabs[0][:, 1, 1:S], in_=pos[:, 1:S], func=ACT.Sin, scale=turns[:, 1:2], bias=math.pi)
+        nc.scalar.copy(out=xs[:].rearrange("p (n t) -> p n t", t=4), in_=spread[:].rearrange("p t n -> p n t"))
 
         beyond = keep.tile([P, S - LATE], F32, name="beyond")
 
@@ -259,7 +260,6 @@ def tile_ropemultiheadattention_pa_kernel(tc, x_bytes, x_scale, Wq, bq, Wk, bk, 
                 nc.sync.dma_start(out=outs[x][b, tt * P:(tt + 1) * P, 2 * P * hf:2 * P * (hf + 1)], in_=resh[:])
 
         fractions()
-        nc.vector.tensor_copy(out=xs[:].rearrange("p (n t) -> p n t", t=4), in_=spread[:].rearrange("p t n -> p n t"))
         cosine_upper()
         for b in range(2):
             for a in range(4):

import math
from contextlib import ExitStack

import concourse.mybir as mybir
from concourse.masks import make_identity

F32 = mybir.dt.float32
BF16 = mybir.dt.bfloat16
U8 = mybir.dt.uint8
U32 = mybir.dt.uint32
I32 = mybir.dt.int32
FP8 = mybir.dt.float8_e4m3fn
FP8X4 = mybir.dt.float8_e4m3fn_x4
ALU = mybir.AluOpType
ACT = mybir.ActivationFunctionType

P = 128
S = 512
FLOPS = 2 * 1024 * 512 * 1024

TWO_PI = 2.0 * math.pi
RATIO = 10000.0 ** (-1.0 / 256.0)

LATE = 448
GROUPS = ((0, 0), (0, 1), (1, 0), (1, 1))
TILES = ((0, 0), (1, 0), (0, 1), (1, 1))
ON_POOL = ((0, 1), (0, 1), (0, 1), (0, 1))


def tile_ropemultiheadattention_pa_kernel(tc, x_bytes, x_scale, Wq, bq, Wk, bk, out_0, out_1):
    nc = tc.nc
    weights = (Wq, Wk)
    biases = (bq, bk)
    outs = (out_0, out_1)

    with ExitStack() as ctx:
        keep = ctx.enter_context(tc.tile_pool(name="keep", bufs=1))
        work = ctx.enter_context(tc.tile_pool(name="work", bufs=3))
        prod = ctx.enter_context(tc.tile_pool(name="prod", bufs=8))
        resp = ctx.enter_context(tc.tile_pool(name="resp", bufs=8))
        psP = ctx.enter_context(tc.psum_pool(name="psP", bufs=5))
        psO = ctx.enter_context(tc.psum_pool(name="psO", bufs=3))
        ctx.enter_context(tc.manual_schedule())

        xs4 = keep.tile([P, 4], F32, name="xs4")
        nc.sync.dma_start(out=xs4[:], in_=x_scale.rearrange("a b (p t) -> (a b p) t", t=4))
        xv = x_bytes.rearrange("b (a p) k -> b p a k", p=P)
        xbytes = [keep.tile([P, 4, 512], U8, name="xbytes%d" % b) for b in range(2)]
        wraw = [keep.tile([P, 4, 512], BF16, name="wraw%d" % x) for x in range(2)]
        nc.sync.dma_start(out=xbytes[0][:], in_=xv[0])
        nc.sync.dma_start(out=wraw[0][:], in_=weights[0].rearrange("(p j) w -> p j w", j=4))
        nc.sync.dma_start(out=xbytes[1][:], in_=xv[1])
        nc.sync.dma_start(out=wraw[1][:], in_=weights[1].rearrange("(p j) w -> p j w", j=4))
        bias = [keep.tile([P, 2, 2], BF16, name="bias%d" % x) for x in range(2)]
        for x in range(2):
            nc.scalar.dma_start(out=bias[x][:], in_=biases[x].rearrange("(h p r) -> p h r", h=2, r=2))

        tabs = [keep.tile([P, 2, S], F32, name="tabs%d" % hf) for hf in range(2)]
        warm = keep.tile([P, 1], F32, name="warm")
        nc.vector.memset(warm[:], 0.0)
        warm2 = keep.tile([P, 1], F32, name="warm2")
        nc.scalar.activation(out=warm2[:], in_=warm[:], func=ACT.Sin)
        ident = keep.tile([P, P], F32, name="ident")
        make_identity(nc, ident[:])
        pos = keep.tile([P, S], F32, name="pos")
        nc.gpsimd.iota(pos[:], pattern=[[1, S]], base=0, channel_multiplier=0, allow_small_or_imprecise_dtypes=True)
        nc.vector.memset(tabs[0][:, 1, 0:1], 0.0)

        xs = keep.tile([P, 512], F32, name="xs")
        spread = psO.tile([P, 4, P], F32, name="spread", tag="O")
        for t in range(4):
            nc.tensor.transpose(spread[:, t, :], xs4[:, t:t + 1].to_broadcast([P, P]), ident[:])

        powers = keep.tile([P, P], F32, name="powers")
        probe = keep.tile([P, 1], F32, name="probe")
        probe_i = keep.tile([P, 1], I32, name="probe_i")
        shift = keep.tile([P, 1], F32, name="shift")
        nc.vector.memset(powers[:, 0:1], 1.0)
        nc.vector.memset(probe[:], 0.75)

        def level(n, count):
            for m in range(1, count + 1):
                nc.vector.tensor_scalar(out=powers[:, m * n:(m + 1) * n], in0=powers[:, 0:n], scalar1=RATIO ** (m * n), scalar2=None, op0=ALU.mult)

        level(1, 3)
        nc.vector.tensor_scalar(out=probe_i[:], in0=probe[:], scalar1=1.0, scalar2=0.0, op0=ALU.mult, op1=ALU.add)
        level(4, 3)
        nc.vector.tensor_scalar(out=shift[:, 0:1], in0=probe_i[:], scalar1=-0.5, scalar2=0.5, op0=ALU.mult, op1=ALU.add)
        level(16, 3)
        level(64, 1)
        diag = keep.tile([P, P], F32, name="diag")
        turns = keep.tile([P, 2], F32, name="turns")
        nc.vector.scalar_tensor_tensor(out=diag[:], in0=powers[:], scalar=1.0 / TWO_PI, in1=ident[:], op0=ALU.mult, op1=ALU.mult, accum_out=turns[:, 0:1])
        nc.vector.tensor_scalar(out=turns[:, 1:2], in0=turns[:, 0:1], scalar1=-TWO_PI * RATIO ** 128, scalar2=None, op0=ALU.mult)

        nc.scalar.activation(out=tabs[0][:, 1, 1:S], in_=pos[:, 1:S], func=ACT.Sin, scale=turns[:, 1:2], bias=math.pi)
        nc.scalar.copy(out=xs[:].rearrange("p (n t) -> p n t", t=4), in_=spread[:].rearrange("p t n -> p n t"))

        beyond = keep.tile([P, S - LATE], F32, name="beyond")

        def cosine_upper():
            nc.scalar.activation(out=tabs[1][:, 0, 0:LATE], in_=pos[:, 0:LATE], func=ACT.Sin, scale=turns[:, 1:2], bias=0.5 * math.pi)
            nc.scalar.activation(out=beyond[:], in_=pos[:, LATE:S], func=ACT.Abs, scale=turns[:, 1:2], bias=math.pi)
            nc.scalar.activation(out=tabs[1][:, 0, LATE:S], in_=beyond[:], func=ACT.Sin, bias=-0.5 * math.pi)

        whole = keep.tile([P, S], I32, name="whole")
        frac = keep.tile([P, S], F32, name="frac")
        folded = keep.tile([P, S], F32, name="folded")

        def fractions():
            nc.vector.tensor_scalar(out=whole[:], in0=pos[:], scalar1=turns[:, 0:1], scalar2=shift[:], op0=ALU.mult, op1=ALU.add)
            nc.vector.scalar_tensor_tensor(out=frac[:], in0=pos[:], scalar=turns[:, 0:1], in1=whole[:], op0=ALU.mult, op1=ALU.subtract)

        def fold():
            nc.scalar.activation(out=folded[:], in_=frac[:], func=ACT.Abs)

        def cosine_lower():
            nc.scalar.activation(out=tabs[0][:, 0, :], in_=folded[:], func=ACT.Sin, scale=-TWO_PI, bias=0.5 * math.pi)

        def sine_lower():
            nc.scalar.activation(out=tabs[1][:, 1, :], in_=frac[:], func=ACT.Sin, scale=-TWO_PI)

        xw = [keep.tile([P, 4, 512], BF16, name="xw%d" % b) for b in range(2)]
        xg = [keep.tile([P, 2048], BF16, name="xg%d" % b, align_bytes=64) for b in range(2)]
        xc = [keep.tile([P, 512], U32, name="xc%d" % b, align_bytes=64) for b in range(2)]
        xsc = [keep.tile([P, 512], U8, name="xsc%d" % b, align_bytes=64) for b in range(2)]
        turned = {}

        def widen(b, a):
            nc.vector.tensor_tensor(out=xw[b][:, a, :], in0=xbytes[b][:, a, :].bitcast(FP8), in1=xs[:], op=ALU.mult)

        def turn_x(b, h):
            if b == 0:
                xt = psO.tile([P, 2, 2, P], F32, name="xt", tag="O")
            else:
                xt = psP.tile([P, 2, 2, P], F32, name="xt1", tag="P")
            for a in range(2):
                words = xw[b][:, 2 * h + a, :].bitcast(F32)
                for u in range(2):
                    nc.tensor.transpose(xt[:, a, u, :], words[:, u:256:2], ident[:])
            turned[(b, h)] = xt

        def take_x(b, h):
            nc.scalar.copy(
                out=xg[b][:].bitcast(F32)[:, h * 512:(h + 1) * 512].rearrange("p (a r u) -> p a r u", a=2, u=2),
                in_=turned[(b, h)][:].rearrange("p a u r -> p a r u"),
            )

        def quant_x(b):
            nc.vector.quantize_mx(out=xc[b][:].bitcast(FP8X4), scales=xsc[b][:], in_=xg[b][:])

        wg = [keep.tile([P, 2048], BF16, name="wg%d" % x, align_bytes=64) for x in range(2)]
        wc = [keep.tile([P, 512], U32, name="wc%d" % x, align_bytes=64) for x in range(2)]
        wsc = [keep.tile([P, 512], U8, name="wsc%d" % x, align_bytes=64) for x in range(2)]

        def prep_w(x, pars=(0, 1)):
            for par in pars:
                for hf in range(2):
                    cb = 2 * par + hf
                    nc.scalar.copy(
                        out=wg[x][:, cb * 512:(cb + 1) * 512].rearrange("p (c i j) -> p c j i", i=4, j=4),
                        in_=wraw[x][:, :, 256 * hf + par:256 * hf + 256:2].rearrange("p j (c i) -> p c j i", i=4),
                    )

        def quant_w(x):
            nc.vector.quantize_mx(out=wc[x][:].bitcast(FP8X4), scales=wsc[x][:], in_=wg[x][:])

        acc = {}
        terms = {}
        banks = {}
        moveds = {}

        def project(g, which):
            x, b = GROUPS[g]
            for par, hf in which:
                cb = 2 * par + hf
                pt = psP.tile([P, S], F32, name="pt", tag="P")
                nc.tensor.matmul_mx(
                    out=pt[:],
                    lhsT=wc[x][:, cb * P:(cb + 1) * P].bitcast(FP8X4),
                    lhsT_scale=wsc[x][:, cb * P:(cb + 1) * P],
                    rhs=xc[b][:].bitcast(FP8X4),
                    rhs_scale=xsc[b][:],
                    start=True,
                    stop=True,
                )
                acc[(g, par, hf)] = pt

        def new_terms(g, par, hf):
            mf = prod.tile([P, 2, S], F32, name="mf", tag="m")
            terms[(g, par, hf)] = mf
            return mf

        def rotate(g, par, hf, lo=0, hi=S):
            x, b = GROUPS[g]
            if lo == 0:
                new_terms(g, par, hf)
            mf = terms[(g, par, hf)]
            nc.vector.scalar_tensor_tensor(
                out=mf[:, :, lo:hi],
                in0=acc[(g, par, hf)][:, lo:hi].unsqueeze(1).to_broadcast([P, 2, hi - lo]),
                scalar=bias[x][:, hf, par:par + 1],
                in1=tabs[hf][:, :, lo:hi],
                op0=ALU.add,
                op1=ALU.mult,
            )

        def move(g, par, hf):
            x, b = GROUPS[g]
            moved = work.tile([P, S], F32, name="moved", tag="moved")
            nc.scalar.activation(out=moved[:], in_=acc[(g, par, hf)][:], func=ACT.Identity, bias=bias[x][:, hf, par:par + 1], scale=1.0)
            moveds[g] = moved

        def rotate_pool(g, par, hf):
            mf = new_terms(g, par, hf)
            for w in ON_POOL[g]:
                nc.gpsimd.tensor_tensor(out=mf[:, w, :], in0=moveds[g][:], in1=tabs[hf][:, w, :], op=ALU.mult)

        def rotate_one(g, par, hf, w):
            x, b = GROUPS[g]
            nc.vector.scalar_tensor_tensor(
                out=terms[(g, par, hf)][:, w, :],
                in0=acc[(g, par, hf)][:],
                scalar=bias[x][:, hf, par:par + 1],
                in1=tabs[hf][:, w, :],
                op0=ALU.add,
                op1=ALU.mult,
            )

        def back(g, par, tt):
            if par == 0:
                banks[(g, tt)] = psO.tile([P, S], F32, name="ot", tag="O")
            ot = banks[(g, tt)]
            for hf in range(2):
                c0 = (2 * hf + par) * P
                nc.tensor.matmul(out=ot[:, c0:c0 + P], lhsT=terms[(g, par, hf)][:, 0, tt * P:(tt + 1) * P], rhs=ident[:], is_transpose=True, start=True, stop=False)
                nc.tensor.matmul(out=ot[:, c0:c0 + P], lhsT=terms[(g, par, 1 - hf)][:, 1, tt * P:(tt + 1) * P], rhs=ident[:], is_transpose=True, start=False, stop=True)

        def store(g, tt, on_vector=False):
            x, b = GROUPS[g]
            res = resp.tile([P, S], F32, name="res", tag="res")
            copy = nc.vector.tensor_copy if on_vector else nc.scalar.copy
            copy(
                out=res[:].rearrange("p (h q r) -> p h q r", h=2, r=2),
                in_=banks[(g, tt)][:].rearrange("p (h r q) -> p h q r", h=2, r=2),
            )
            nc.sync.dma_start(out=outs[x][b, tt * P:(tt + 1) * P, :], in_=res[:])

        def last_tile(g, tt):
            x, b = GROUPS[g]
            for hf in range(2):
                oh = psO.tile([P, 2 * P], F32, name="oh", tag="O")
                for par in range(2):
                    c0 = par * P
                    nc.tensor.matmul(out=oh[:, c0:c0 + P], lhsT=terms[(g, par, hf)][:, 0, tt * P:(tt + 1) * P], rhs=ident[:], is_transpose=True, start=True, stop=False)
                    nc.tensor.matmul(out=oh[:, c0:c0 + P], lhsT=terms[(g, par, 1 - hf)][:, 1, tt * P:(tt + 1) * P], rhs=ident[:], is_transpose=True, start=False, stop=True)
                resh = resp.tile([P, 2 * P], F32, name="resh", tag="res")
                copy = nc.vector.tensor_copy if hf == 1 else nc.scalar.copy
                copy(out=resh[:].rearrange("p (q r) -> p q r", r=2), in_=oh[:].rearrange("p (r q) -> p q r", r=2))
                nc.sync.dma_start(out=outs[x][b, tt * P:(tt + 1) * P, 2 * P * hf:2 * P * (hf + 1)], in_=resh[:])

        fractions()
        cosine_upper()
        for b in range(2):
            for a in range(4):
                widen(b, a)
                if a % 2 == 1:
                    turn_x(b, a // 2)
        prep_w(0)
        take_x(0, 0)
        fold()
        take_x(0, 1)
        cosine_lower()
        take_x(1, 0)
        take_x(1, 1)
        sine_lower()
        quant_w(0)
        quant_x(0)
        project(0, TILES)
        quant_x(1)

        move(0, 1, 0)
        for g in range(4):
            rotate_pool(g, 1, 0)
            rotate(g, 0, 0)
            if g == 0:
                prep_w(1, (0,))
                project(1, TILES[0:3])
                move(1, 1, 0)
                prep_w(1, (1,))
            if g == 1:
                quant_w(1)
            rotate(g, 0, 1)
            if g == 0:
                project(1, TILES[3:4])
            elif g < 3:
                project(g + 1, TILES)
                move(g + 1, 1, 0)
            rotate(g, 1, 1)
            for tt in range(4):
                if g == 3 and tt == 3:
                    last_tile(g, tt)
                else:
                    back(g, 0, tt)
                    back(g, 1, tt)
                    store(g, tt)
